import numpy as np
import ml_dtypes

BF16 = ml_dtypes.bfloat16


def bf(x):
    return np.asarray(x, np.float32).astype(BF16)


def f32(x):
    return np.asarray(x, np.float32)


def f64(x):
    return np.asarray(x).astype(np.float64)


def striped(idx):
    return np.tile(idx.reshape(-1, 16).T, (8, 1))


D, V, B, T, N, M = 512, 2048, 4, 128, 512, 1536


def sinusoidal(t, d):
    pos = np.arange(t, dtype=np.float32)[:, None]
    div = np.exp(np.arange(0, d, 2).astype(np.float32) * np.float32(-np.log(10000.0) / d))
    ang = f64(pos * div)
    pe = np.zeros((t, d))
    pe[:, 0::2] = np.sin(ang)
    pe[:, 1::2] = np.cos(ang)
    return pe


def setup_inputs():
    return {"emb": f32(np.random.standard_normal((D, V))), "pe": f32(np.tile(sinusoidal(T, D).T, (1, B))), "qkv_w": bf(np.random.standard_normal((D, M)) / np.sqrt(D)), "qkv_b": f32(0.1 * np.random.standard_normal((M, 1))), "offs": striped(np.random.permutation(np.tile(np.arange(V), 2))[:N])}


def reference(emb, pe, qkv_w, qkv_b, offs):
    idx = offs[:16].T.reshape(-1)
    x = f64(emb)[:, idx] + f64(pe)
    qkv = f64(qkv_w).T @ x + f64(qkv_b)
    return np.concatenate([x, qkv], axis=0)

@@ -1,0 +1,67 @@
+import concourse.mybir as mybir
+from concourse.masks import make_identity
+
+P = 128
+D, V, N, M = 512, 2048, 512, 1536
+C_BLOCKS = D // P
+M_BLOCKS = M // P
+F32, BF16, U16 = mybir.dt.float32, mybir.dt.bfloat16, mybir.dt.uint16
+ADD = mybir.AluOpType.add
+IDENTITY = mybir.ActivationFunctionType.Identity
+
+FLOPS = 2 * D * M * N
+
+
+def tile_attentionbasedmodel_kernel(tc, emb, pe, qkv_w, qkv_b, offs, out):
+    nc = tc.nc
+    with (
+        tc.tile_pool(name="held", bufs=1) as held,
+        tc.psum_pool(name="flip", bufs=1) as flip,
+        tc.psum_pool(name="banks", bufs=4) as banks,
+    ):
+        offsets = held.tile([P, N // 16], U16, name="offsets")
+        nc.sync.dma_start(offsets[:], offs)
+        table, pos, weights = [], [], []
+        for c in range(C_BLOCKS):
+            rows = slice(c * P, (c + 1) * P)
+            table.append(held.tile([P, V], F32, name=f"table{c}"))
+            pos.append(held.tile([P, N], F32, name=f"pos{c}"))
+            weights.append(held.tile([P, M], BF16, name=f"weights{c}"))
+            nc.sync.dma_start(table[c][:], emb[rows, :])
+            nc.sync.dma_start(pos[c][:], pe[rows, :])
+            nc.sync.dma_start(weights[c][:], qkv_w[rows, :])
+
+        bias_rows = held.tile([P, P], F32, name="bias_rows")
+        nc.gpsimd.memset(bias_rows[:], 0.0)
+        nc.sync.dma_start(bias_rows[0:M_BLOCKS, :], qkv_b.rearrange("(b p) o -> b (p o)", p=P))
+        identity = held.tile([P, P], F32, name="identity")
+        make_identity(nc, identity[:])
+        bias_flipped = flip.tile([P, P], F32, name="bias_flipped")
+        nc.tensor.transpose(bias_flipped[:], bias_rows[:], identity[:])
+        bias = held.tile([P, M_BLOCKS], F32, name="bias")
+        nc.vector.tensor_copy(bias[:], bias_flipped[:, 0:M_BLOCKS])
+
+        x_bf16 = []
+        for c in range(C_BLOCKS):
+            x = held.tile([P, N], F32, name=f"x{c}")
+            nc.vector.tensor_tensor(x[:], table[c][:].indirect(offsets[:]), pos[c][:], ADD)
+            nc.sync.dma_start(out[c * P : (c + 1) * P, :], x[:])
+            x_bf16.append(held.tile([P, N], BF16, name=f"x_bf16_{c}"))
+            nc.vector.tensor_copy(x_bf16[c][:], x[:])
+
+        for m in range(M_BLOCKS):
+            acc = banks.tile([P, N], F32, name="acc")
+            for c in range(C_BLOCKS):
+                nc.tensor.matmul(
+                    acc[:],
+                    weights[c][:, m * P : (m + 1) * P],
+                    x_bf16[c][:],
+                    start=(c == 0),
+                    stop=(c == C_BLOCKS - 1),
+                )
+            qkv = held.tile([P, N], F32, name=f"qkv{m}")
+            if m % 2 == 0:
+                nc.scalar.activation(qkv[:], acc[:], IDENTITY, bias=bias[:, m : m + 1])
+            else:
+                nc.vector.tensor_scalar_add(qkv[:], acc[:], bias[:, m : m + 1])
+            nc.sync.dma_start(out[D + m * P : D + (m + 1) * P, :], qkv[:])

@@ -1,10 +1,9 @@
 import concourse.mybir as mybir
-from concourse.masks import make_identity
 
 P = 128
 D, V, N, M = 512, 2048, 512, 1536
-C_BLOCKS = D // P
-M_BLOCKS = M // P
+R = D // P
+QKV = M // D
 F32, BF16, U16 = mybir.dt.float32, mybir.dt.bfloat16, mybir.dt.uint16
 ADD = mybir.AluOpType.add
 IDENTITY = mybir.ActivationFunctionType.Identity
@@ -14,54 +13,62 @@ FLOPS = 2 * D * M * N
 
 def tile_attentionbasedmodel_kernel(tc, emb, pe, qkv_w, qkv_b, offs, out):
     nc = tc.nc
+    emb_rows = emb.rearrange("(p b) v -> p b v", b=R)
+    pe_rows = pe.rearrange("(p b) j -> p b j", b=R)
+    w_rows = qkv_w.rearrange("(p b) m -> p b m", b=R)
+    bias_rows = qkv_b.rearrange("(g p b) o -> p g (b o)", g=QKV, b=R)
+    out_rows = out.rearrange("(g p b) j -> g p b j", g=1 + QKV, b=R)
+
     with (
         tc.tile_pool(name="held", bufs=1) as held,
-        tc.psum_pool(name="flip", bufs=1) as flip,
-        tc.psum_pool(name="banks", bufs=4) as banks,
+        tc.psum_pool(name="banks", bufs=8) as banks,
     ):
         offsets = held.tile([P, N // 16], U16, name="offsets")
         nc.sync.dma_start(offsets[:], offs)
-        table, pos, weights = [], [], []
-        for c in range(C_BLOCKS):
-            rows = slice(c * P, (c + 1) * P)
-            table.append(held.tile([P, V], F32, name=f"table{c}"))
-            pos.append(held.tile([P, N], F32, name=f"pos{c}"))
-            weights.append(held.tile([P, M], BF16, name=f"weights{c}"))
-            nc.sync.dma_start(table[c][:], emb[rows, :])
-            nc.sync.dma_start(pos[c][:], pe[rows, :])
-            nc.sync.dma_start(weights[c][:], qkv_w[rows, :])
+        table = [held.tile([P, V], F32, name=f"table{c}") for c in range(R)]
+        pos = held.tile([P, R, N], F32, name="pos")
+        w_qk = held.tile([P, R, 2 * D], BF16, name="w_qk")
+        w_v = held.tile([P, R, D], BF16, name="w_v")
+        bias = held.tile([P, QKV, R], F32, name="bias")
+        nc.sync.dma_start(table[0][:], emb_rows[:, 0, :])
+        nc.sync.dma_start(pos[:], pe_rows)
+        nc.sync.dma_start(w_qk[:], w_rows[:, :, 0 : 2 * D])
+        nc.sync.dma_start(bias[:], bias_rows)
+        for c in range(1, R):
+            nc.sync.dma_start(table[c][:], emb_rows[:, c, :])
+        nc.sync.dma_start(w_v[:], w_rows[:, :, 2 * D : 3 * D])
 
-        bias_rows = held.tile([P, P], F32, name="bias_rows")
-        nc.gpsimd.memset(bias_rows[:], 0.0)
-        nc.sync.dma_start(bias_rows[0:M_BLOCKS, :], qkv_b.rearrange("(b p) o -> b (p o)", p=P))
-        identity = held.tile([P, P], F32, name="identity")
-        make_identity(nc, identity[:])
-        bias_flipped = flip.tile([P, P], F32, name="bias_flipped")
-        nc.tensor.transpose(bias_flipped[:], bias_rows[:], identity[:])
-        bias = held.tile([P, M_BLOCKS], F32, name="bias")
-        nc.vector.tensor_copy(bias[:], bias_flipped[:, 0:M_BLOCKS])
+        qk_blocks = w_qk[:].rearrange("p c (g q b) -> p c g b q", g=2, b=R)
+        v_blocks = w_v[:].rearrange("p c (q b) -> p c b q", b=R)
 
-        x_bf16 = []
-        for c in range(C_BLOCKS):
-            x = held.tile([P, N], F32, name=f"x{c}")
-            nc.vector.tensor_tensor(x[:], table[c][:].indirect(offsets[:]), pos[c][:], ADD)
-            nc.sync.dma_start(out[c * P : (c + 1) * P, :], x[:])
-            x_bf16.append(held.tile([P, N], BF16, name=f"x_bf16_{c}"))
-            nc.vector.tensor_copy(x_bf16[c][:], x[:])
+        x = held.tile([P, R, N], F32, name="x")
+        x_bf16 = held.tile([P, R, N], BF16, name="x_bf16")
+        qkv = [held.tile([P, R, N], F32, name=f"qkv{g}") for g in range(QKV)]
 
-        for m in range(M_BLOCKS):
-            acc = banks.tile([P, N], F32, name="acc")
-            for c in range(C_BLOCKS):
-                nc.tensor.matmul(
-                    acc[:],
-                    weights[c][:, m * P : (m + 1) * P],
-                    x_bf16[c][:],
-                    start=(c == 0),
-                    stop=(c == C_BLOCKS - 1),
-                )
-            qkv = held.tile([P, N], F32, name=f"qkv{m}")
-            if m % 2 == 0:
-                nc.scalar.activation(qkv[:], acc[:], IDENTITY, bias=bias[:, m : m + 1])
+        def leave_psum(acc, g, b):
+            if b % 2 == 0:
+                nc.scalar.activation(qkv[g][:, b, :], acc[:], IDENTITY, bias=bias[:, g, b : b + 1])
             else:
-                nc.vector.tensor_scalar_add(qkv[:], acc[:], bias[:, m : m + 1])
-            nc.sync.dma_start(out[D + m * P : D + (m + 1) * P, :], qkv[:])
+                nc.vector.tensor_scalar_add(qkv[g][:, b, :], acc[:], bias[:, g, b : b + 1])
+                nc.sync.dma_start(out_rows[1 + g, :, b - 1 : b + 1, :], qkv[g][:, b - 1 : b + 1, :])
+
+        qk_acc = [[banks.tile([P, N], F32, name=f"acc{g}{b}", tag="acc") for b in range(R)] for g in range(2)]
+        for c in range(R):
+            nc.vector.tensor_tensor(x[:, c, :], table[c][:].indirect(offsets[:]), pos[:, c, :], ADD)
+            nc.vector.tensor_copy(x_bf16[:, c, :], x[:, c, :])
+            if c % 2 == 1:
+                nc.sync.dma_start(out_rows[0, :, c - 1 : c + 1, :], x[:, c - 1 : c + 1, :])
+            for g in range(2):
+                for b in range(R):
+                    nc.tensor.matmul(
+                        qk_acc[g][b][:], qk_blocks[:, c, g, b, :], x_bf16[:, c, :], start=(c == 0), stop=(c == R - 1)
+                    )
+        for g in range(2):
+            for b in range(R):
+                leave_psum(qk_acc[g][b], g, b)
+
+        for b in range(R):
+            v_acc = banks.tile([P, N], F32, name=f"acc2{b}", tag="acc")
+            for c in range(R):
+                nc.tensor.matmul(v_acc[:], v_blocks[:, c, b, :], x_bf16[:, c, :], start=(c == 0), stop=(c == R - 1))
+            leave_psum(v_acc, 2, b)

@@ -26,19 +26,18 @@ def tile_attentionbasedmodel_kernel(tc, emb, pe, qkv_w, qkv_b, offs, out):
         offsets = held.tile([P, N // 16], U16, name="offsets")
         nc.sync.dma_start(offsets[:], offs)
         table = [held.tile([P, V], F32, name=f"table{c}") for c in range(R)]
-        pos = held.tile([P, R, N], F32, name="pos")
-        w_qk = held.tile([P, R, 2 * D], BF16, name="w_qk")
+        pos = [held.tile([P, N], F32, name=f"pos{c}") for c in range(R)]
+        w_qk = [held.tile([P, 2 * D], BF16, name=f"w_qk{c}") for c in range(R)]
         w_v = held.tile([P, R, D], BF16, name="w_v")
         bias = held.tile([P, QKV, R], F32, name="bias")
-        nc.sync.dma_start(table[0][:], emb_rows[:, 0, :])
-        nc.sync.dma_start(pos[:], pe_rows)
-        nc.sync.dma_start(w_qk[:], w_rows[:, :, 0 : 2 * D])
-        nc.sync.dma_start(bias[:], bias_rows)
-        for c in range(1, R):
+        for c in range(R):
             nc.sync.dma_start(table[c][:], emb_rows[:, c, :])
+            nc.sync.dma_start(pos[c][:], pe_rows[:, c, :])
+            nc.sync.dma_start(w_qk[c][:], w_rows[:, c, 0 : 2 * D])
+        nc.sync.dma_start(bias[:], bias_rows)
         nc.sync.dma_start(w_v[:], w_rows[:, :, 2 * D : 3 * D])
 
-        qk_blocks = w_qk[:].rearrange("p c (g q b) -> p c g b q", g=2, b=R)
+        qk_blocks = [w_qk[c][:].rearrange("p (g q b) -> p g b q", g=2, b=R) for c in range(R)]
         v_blocks = w_v[:].rearrange("p c (q b) -> p c b q", b=R)
 
         x = held.tile([P, R, N], F32, name="x")
@@ -54,14 +53,14 @@ def tile_attentionbasedmodel_kernel(tc, emb, pe, qkv_w, qkv_b, offs, out):
 
         qk_acc = [[banks.tile([P, N], F32, name=f"acc{g}{b}", tag="acc") for b in range(R)] for g in range(2)]
         for c in range(R):
-            nc.vector.tensor_tensor(x[:, c, :], table[c][:].indirect(offsets[:]), pos[:, c, :], ADD)
+            nc.vector.tensor_tensor(x[:, c, :], table[c][:].indirect(offsets[:]), pos[c][:], ADD)
             nc.vector.tensor_copy(x_bf16[:, c, :], x[:, c, :])
             if c % 2 == 1:
                 nc.sync.dma_start(out_rows[0, :, c - 1 : c + 1, :], x[:, c - 1 : c + 1, :])
             for g in range(2):
                 for b in range(R):
                     nc.tensor.matmul(
-                        qk_acc[g][b][:], qk_blocks[:, c, g, b, :], x_bf16[:, c, :], start=(c == 0), stop=(c == R - 1)
+                        qk_acc[g][b][:], qk_blocks[c][:, g, b, :], x_bf16[:, c, :], start=(c == 0), stop=(c == R - 1)
                     )
         for g in range(2):
             for b in range(R):

@@ -49,7 +49,7 @@ def tile_attentionbasedmodel_kernel(tc, emb, pe, qkv_w, qkv_b, offs, out):
                 nc.scalar.activation(qkv[g][:, b, :], acc[:], IDENTITY, bias=bias[:, g, b : b + 1])
             else:
                 nc.vector.tensor_scalar_add(qkv[g][:, b, :], acc[:], bias[:, g, b : b + 1])
-                nc.sync.dma_start(out_rows[1 + g, :, b - 1 : b + 1, :], qkv[g][:, b - 1 : b + 1, :])
+            nc.sync.dma_start(out_rows[1 + g, :, b, :], qkv[g][:, b, :])
 
         qk_acc = [[banks.tile([P, N], F32, name=f"acc{g}{b}", tag="acc") for b in range(R)] for g in range(2)]
         for c in range(R):

@@ -53,15 +53,24 @@ def tile_attentionbasedmodel_kernel(tc, emb, pe, qkv_w, qkv_b, offs, out):
 
         qk_acc = [[banks.tile([P, N], F32, name=f"acc{g}{b}", tag="acc") for b in range(R)] for g in range(2)]
         for c in range(R):
-            nc.vector.tensor_tensor(x[:, c, :], table[c][:].indirect(offsets[:]), pos[c][:], ADD)
-            nc.vector.tensor_copy(x_bf16[:, c, :], x[:, c, :])
+            pieces = 2 if c == R - 1 else 1
+            width = N // pieces
+            for h in range(pieces):
+                tokens = slice(h * width, (h + 1) * width)
+                piece = offsets[:, h * width // 16 : (h + 1) * width // 16]
+                nc.vector.tensor_tensor(x[:, c, tokens], table[c][:].indirect(piece), pos[c][:, tokens], ADD)
+                nc.vector.tensor_copy(x_bf16[:, c, tokens], x[:, c, tokens])
+                for g in range(2):
+                    for b in range(R):
+                        nc.tensor.matmul(
+                            qk_acc[g][b][:, tokens],
+                            qk_blocks[c][:, g, b, :],
+                            x_bf16[:, c, tokens],
+                            start=(c == 0),
+                            stop=(c == R - 1 and h == pieces - 1),
+                        )
             if c % 2 == 1:
                 nc.sync.dma_start(out_rows[0, :, c - 1 : c + 1, :], x[:, c - 1 : c + 1, :])
-            for g in range(2):
-                for b in range(R):
-                    nc.tensor.matmul(
-                        qk_acc[g][b][:], qk_blocks[c][:, g, b, :], x_bf16[:, c, :], start=(c == 0), stop=(c == R - 1)
-                    )
         for g in range(2):
             for b in range(R):
                 leave_psum(qk_acc[g][b], g, b)

@@ -25,16 +25,16 @@ def tile_attentionbasedmodel_kernel(tc, emb, pe, qkv_w, qkv_b, offs, out):
     ):
         offsets = held.tile([P, N // 16], U16, name="offsets")
         nc.sync.dma_start(offsets[:], offs)
+        bias = held.tile([P, QKV, R], F32, name="bias")
+        nc.scalar.dma_start(bias[:], bias_rows)
         table = [held.tile([P, V], F32, name=f"table{c}") for c in range(R)]
         pos = [held.tile([P, N], F32, name=f"pos{c}") for c in range(R)]
         w_qk = [held.tile([P, 2 * D], BF16, name=f"w_qk{c}") for c in range(R)]
         w_v = held.tile([P, R, D], BF16, name="w_v")
-        bias = held.tile([P, QKV, R], F32, name="bias")
         for c in range(R):
             nc.sync.dma_start(table[c][:], emb_rows[:, c, :])
             nc.sync.dma_start(pos[c][:], pe_rows[:, c, :])
             nc.sync.dma_start(w_qk[c][:], w_rows[:, c, 0 : 2 * D])
-        nc.sync.dma_start(bias[:], bias_rows)
         nc.sync.dma_start(w_v[:], w_rows[:, :, 2 * D : 3 * D])
 
         qk_blocks = [w_qk[c][:].rearrange("p (g q b) -> p g b q", g=2, b=R) for c in range(R)]
@@ -53,24 +53,15 @@ def tile_attentionbasedmodel_kernel(tc, emb, pe, qkv_w, qkv_b, offs, out):
 
         qk_acc = [[banks.tile([P, N], F32, name=f"acc{g}{b}", tag="acc") for b in range(R)] for g in range(2)]
         for c in range(R):
-            pieces = 2 if c == R - 1 else 1
-            width = N // pieces
-            for h in range(pieces):
-                tokens = slice(h * width, (h + 1) * width)
-                piece = offsets[:, h * width // 16 : (h + 1) * width // 16]
-                nc.vector.tensor_tensor(x[:, c, tokens], table[c][:].indirect(piece), pos[c][:, tokens], ADD)
-                nc.vector.tensor_copy(x_bf16[:, c, tokens], x[:, c, tokens])
-                for g in range(2):
-                    for b in range(R):
-                        nc.tensor.matmul(
-                            qk_acc[g][b][:, tokens],
-                            qk_blocks[c][:, g, b, :],
-                            x_bf16[:, c, tokens],
-                            start=(c == 0),
-                            stop=(c == R - 1 and h == pieces - 1),
-                        )
+            nc.vector.tensor_tensor(x[:, c, :], table[c][:].indirect(offsets[:]), pos[c][:], ADD)
+            nc.vector.tensor_copy(x_bf16[:, c, :], x[:, c, :])
             if c % 2 == 1:
                 nc.sync.dma_start(out_rows[0, :, c - 1 : c + 1, :], x[:, c - 1 : c + 1, :])
+            for g in range(2):
+                for b in range(R):
+                    nc.tensor.matmul(
+                        qk_acc[g][b][:], qk_blocks[c][:, g, b, :], x_bf16[:, c, :], start=(c == 0), stop=(c == R - 1)
+                    )
         for g in range(2):
             for b in range(R):
                 leave_psum(qk_acc[g][b], g, b)

@@ -2,8 +2,10 @@ import concourse.mybir as mybir
 
 P = 128
 D, V, N, M = 512, 2048, 512, 1536
-R = D // P
-QKV = M // D
+BLOCKS = D // P
+GROUP_Q, GROUP_K, GROUP_V = 0, 1, 2
+PSUM_BANKS = 8
+OFFSETS_A_COLUMN = 16
 F32, BF16, U16 = mybir.dt.float32, mybir.dt.bfloat16, mybir.dt.uint16
 ADD = mybir.AluOpType.add
 IDENTITY = mybir.ActivationFunctionType.Identity
@@ -13,61 +15,69 @@ FLOPS = 2 * D * M * N
 
 def tile_attentionbasedmodel_kernel(tc, emb, pe, qkv_w, qkv_b, offs, out):
     nc = tc.nc
-    emb_rows = emb.rearrange("(p b) v -> p b v", b=R)
-    pe_rows = pe.rearrange("(p b) j -> p b j", b=R)
-    w_rows = qkv_w.rearrange("(p b) m -> p b m", b=R)
-    bias_rows = qkv_b.rearrange("(g p b) o -> p g (b o)", g=QKV, b=R)
-    out_rows = out.rearrange("(g p b) j -> g p b j", g=1 + QKV, b=R)
+    emb_blocks = emb.rearrange("(p i) v -> p i v", i=BLOCKS)
+    pe_blocks = pe.rearrange("(p i) j -> p i j", i=BLOCKS)
+    w_blocks = qkv_w.rearrange("(p i) m -> p i m", i=BLOCKS)
+    bias_blocks = qkv_b.rearrange("(g p i) o -> p g (i o)", p=P, i=BLOCKS)
+    out_blocks = out.rearrange("(g p i) j -> g p i j", p=P, i=BLOCKS)
 
     with (
         tc.tile_pool(name="held", bufs=1) as held,
-        tc.psum_pool(name="banks", bufs=8) as banks,
+        tc.psum_pool(name="banks", bufs=PSUM_BANKS) as banks,
     ):
-        offsets = held.tile([P, N // 16], U16, name="offsets")
+        offsets = held.tile([P, N // OFFSETS_A_COLUMN], U16, name="offsets")
         nc.sync.dma_start(offsets[:], offs)
-        bias = held.tile([P, QKV, R], F32, name="bias")
-        nc.scalar.dma_start(bias[:], bias_rows)
-        table = [held.tile([P, V], F32, name=f"table{c}") for c in range(R)]
-        pos = [held.tile([P, N], F32, name=f"pos{c}") for c in range(R)]
-        w_qk = [held.tile([P, 2 * D], BF16, name=f"w_qk{c}") for c in range(R)]
-        w_v = held.tile([P, R, D], BF16, name="w_v")
-        for c in range(R):
-            nc.sync.dma_start(table[c][:], emb_rows[:, c, :])
-            nc.sync.dma_start(pos[c][:], pe_rows[:, c, :])
-            nc.sync.dma_start(w_qk[c][:], w_rows[:, c, 0 : 2 * D])
-        nc.sync.dma_start(w_v[:], w_rows[:, :, 2 * D : 3 * D])
+        table = [held.tile([P, V], F32, name=f"table{cb}") for cb in range(BLOCKS)]
+        pos = [held.tile([P, N], F32, name=f"pos{cb}") for cb in range(BLOCKS)]
+        w_qk = [held.tile([P, 2 * D], BF16, name=f"w_qk{cb}") for cb in range(BLOCKS)]
+        w_v = held.tile([P, BLOCKS, D], BF16, name="w_v")
+        bias = held.tile([P, M // D, BLOCKS], F32, name="bias")
+        for cb in range(BLOCKS):
+            nc.sync.dma_start(table[cb][:], emb_blocks[:, cb, :])
+            nc.sync.dma_start(pos[cb][:], pe_blocks[:, cb, :])
+            nc.sync.dma_start(w_qk[cb][:], w_blocks[:, cb, 0 : 2 * D])
+        nc.sync.dma_start(bias[:], bias_blocks)
+        nc.sync.dma_start(w_v[:], w_blocks[:, :, 2 * D : M])
 
-        qk_blocks = [w_qk[c][:].rearrange("p (g q b) -> p g b q", g=2, b=R) for c in range(R)]
-        v_blocks = w_v[:].rearrange("p c (q b) -> p c b q", b=R)
+        w_qk_blocks = [w_qk[cb][:].rearrange("p (g f i) -> p g i f", g=2, i=BLOCKS) for cb in range(BLOCKS)]
+        w_v_blocks = w_v[:].rearrange("p c (f i) -> p c i f", i=BLOCKS)
 
-        x = held.tile([P, R, N], F32, name="x")
-        x_bf16 = held.tile([P, R, N], BF16, name="x_bf16")
-        qkv = [held.tile([P, R, N], F32, name=f"qkv{g}") for g in range(QKV)]
+        x = held.tile([P, BLOCKS, N], F32, name="x")
+        x_bf16 = held.tile([P, BLOCKS, N], BF16, name="x_bf16")
+        qkv = [held.tile([P, BLOCKS, N], F32, name=f"qkv{g}") for g in (GROUP_Q, GROUP_K, GROUP_V)]
 
-        def leave_psum(acc, g, b):
-            if b % 2 == 0:
-                nc.scalar.activation(qkv[g][:, b, :], acc[:], IDENTITY, bias=bias[:, g, b : b + 1])
+        def add_bias_and_store(acc, g, fb):
+            if fb % 2 == 0:
+                nc.scalar.activation(qkv[g][:, fb, :], acc[:], IDENTITY, bias=bias[:, g, fb : fb + 1])
             else:
-                nc.vector.tensor_scalar_add(qkv[g][:, b, :], acc[:], bias[:, g, b : b + 1])
-            nc.sync.dma_start(out_rows[1 + g, :, b, :], qkv[g][:, b, :])
+                nc.vector.tensor_scalar_add(qkv[g][:, fb, :], acc[:], bias[:, g, fb : fb + 1])
+            nc.sync.dma_start(out_blocks[1 + g, :, fb, :], qkv[g][:, fb, :])
 
-        qk_acc = [[banks.tile([P, N], F32, name=f"acc{g}{b}", tag="acc") for b in range(R)] for g in range(2)]
-        for c in range(R):
-            nc.vector.tensor_tensor(x[:, c, :], table[c][:].indirect(offsets[:]), pos[c][:], ADD)
-            nc.vector.tensor_copy(x_bf16[:, c, :], x[:, c, :])
-            if c % 2 == 1:
-                nc.sync.dma_start(out_rows[0, :, c - 1 : c + 1, :], x[:, c - 1 : c + 1, :])
-            for g in range(2):
-                for b in range(R):
+        qk_acc = [
+            [banks.tile([P, N], F32, name=f"acc{g}{fb}", tag="acc") for fb in range(BLOCKS)]
+            for g in (GROUP_Q, GROUP_K)
+        ]
+        for cb in range(BLOCKS):
+            nc.vector.tensor_tensor(x[:, cb, :], table[cb][:].indirect(offsets[:]), pos[cb][:], ADD)
+            nc.vector.tensor_copy(x_bf16[:, cb, :], x[:, cb, :])
+            nc.sync.dma_start(out_blocks[0, :, cb, :], x[:, cb, :])
+            for g in (GROUP_Q, GROUP_K):
+                for fb in range(BLOCKS):
                     nc.tensor.matmul(
-                        qk_acc[g][b][:], qk_blocks[c][:, g, b, :], x_bf16[:, c, :], start=(c == 0), stop=(c == R - 1)
+                        qk_acc[g][fb][:],
+                        w_qk_blocks[cb][:, g, fb, :],
+                        x_bf16[:, cb, :],
+                        start=(cb == 0),
+                        stop=(cb == BLOCKS - 1),
                     )
-        for g in range(2):
-            for b in range(R):
-                leave_psum(qk_acc[g][b], g, b)
+        for g in (GROUP_Q, GROUP_K):
+            for fb in range(BLOCKS):
+                add_bias_and_store(qk_acc[g][fb], g, fb)
 
-        for b in range(R):
-            v_acc = banks.tile([P, N], F32, name=f"acc2{b}", tag="acc")
-            for c in range(R):
-                nc.tensor.matmul(v_acc[:], v_blocks[:, c, b, :], x_bf16[:, c, :], start=(c == 0), stop=(c == R - 1))
-            leave_psum(v_acc, 2, b)
+        for fb in range(BLOCKS):
+            v_acc = banks.tile([P, N], F32, name=f"acc{GROUP_V}{fb}", tag="acc")
+            for cb in range(BLOCKS):
+                nc.tensor.matmul(
+                    v_acc[:], w_v_blocks[:, cb, fb, :], x_bf16[:, cb, :], start=(cb == 0), stop=(cb == BLOCKS - 1)
+                )
+            add_bias_and_store(v_acc, GROUP_V, fb)

@@ -2,6 +2,7 @@ import concourse.mybir as mybir
 
 P = 128
 D, V, N, M = 512, 2048, 512, 1536
+T = 128
 BLOCKS = D // P
 GROUP_Q, GROUP_K, GROUP_V = 0, 1, 2
 PSUM_BANKS = 8
@@ -11,6 +12,7 @@ ADD = mybir.AluOpType.add
 IDENTITY = mybir.ActivationFunctionType.Identity
 
 FLOPS = 2 * D * M * N
+BYTES = 4 * D * V + 4 * D * T + 2 * D * M + 4 * M + 2 * P * (N // OFFSETS_A_COLUMN) + 4 * (D + M) * N
 
 
 def tile_attentionbasedmodel_kernel(tc, emb, pe, qkv_w, qkv_b, offs, out):
@@ -28,13 +30,13 @@ def tile_attentionbasedmodel_kernel(tc, emb, pe, qkv_w, qkv_b, offs, out):
         offsets = held.tile([P, N // OFFSETS_A_COLUMN], U16, name="offsets")
         nc.sync.dma_start(offsets[:], offs)
         table = [held.tile([P, V], F32, name=f"table{cb}") for cb in range(BLOCKS)]
-        pos = [held.tile([P, N], F32, name=f"pos{cb}") for cb in range(BLOCKS)]
+        pos = held.tile([P, BLOCKS, T], F32, name="pos")
+        nc.sync.dma_start(pos[:], pe_blocks[:, :, 0:T])
         w_qk = [held.tile([P, 2 * D], BF16, name=f"w_qk{cb}") for cb in range(BLOCKS)]
         w_v = held.tile([P, BLOCKS, D], BF16, name="w_v")
         bias = held.tile([P, M // D, BLOCKS], F32, name="bias")
         for cb in range(BLOCKS):
             nc.sync.dma_start(table[cb][:], emb_blocks[:, cb, :])
-            nc.sync.dma_start(pos[cb][:], pe_blocks[:, cb, :])
             nc.sync.dma_start(w_qk[cb][:], w_blocks[:, cb, 0 : 2 * D])
         nc.sync.dma_start(bias[:], bias_blocks)
         nc.sync.dma_start(w_v[:], w_blocks[:, :, 2 * D : M])
@@ -58,7 +60,11 @@ def tile_attentionbasedmodel_kernel(tc, emb, pe, qkv_w, qkv_b, offs, out):
             for g in (GROUP_Q, GROUP_K)
         ]
         for cb in range(BLOCKS):
-            nc.vector.tensor_tensor(x[:, cb, :], table[cb][:].indirect(offsets[:]), pos[cb][:], ADD)
+            for s in range(N // T):
+                piece = offsets[:, s * (T // OFFSETS_A_COLUMN) : (s + 1) * (T // OFFSETS_A_COLUMN)]
+                nc.vector.tensor_tensor(
+                    x[:, cb, s * T : (s + 1) * T], table[cb][:].indirect(piece), pos[:, cb, :], ADD
+                )
             nc.vector.tensor_copy(x_bf16[:, cb, :], x[:, cb, :])
             nc.sync.dma_start(out_blocks[0, :, cb, :], x[:, cb, :])
             for g in (GROUP_Q, GROUP_K):

@@ -48,12 +48,14 @@ def tile_attentionbasedmodel_kernel(tc, emb, pe, qkv_w, qkv_b, offs, out):
         x_bf16 = held.tile([P, BLOCKS, N], BF16, name="x_bf16")
         qkv = [held.tile([P, BLOCKS, N], F32, name=f"qkv{g}") for g in (GROUP_Q, GROUP_K, GROUP_V)]
 
-        def add_bias_and_store(acc, g, fb):
+        def add_bias(acc, g, fb):
             if fb % 2 == 0:
                 nc.scalar.activation(qkv[g][:, fb, :], acc[:], IDENTITY, bias=bias[:, g, fb : fb + 1])
             else:
                 nc.vector.tensor_scalar_add(qkv[g][:, fb, :], acc[:], bias[:, g, fb : fb + 1])
-            nc.sync.dma_start(out_blocks[1 + g, :, fb, :], qkv[g][:, fb, :])
+
+        def store(g, first, count):
+            nc.sync.dma_start(out_blocks[1 + g, :, first : first + count, :], qkv[g][:, first : first + count, :])
 
         qk_acc = [
             [banks.tile([P, N], F32, name=f"acc{g}{fb}", tag="acc") for fb in range(BLOCKS)]
@@ -66,7 +68,10 @@ def tile_attentionbasedmodel_kernel(tc, emb, pe, qkv_w, qkv_b, offs, out):
                     x[:, cb, s * T : (s + 1) * T], table[cb][:].indirect(piece), pos[:, cb, :], ADD
                 )
             nc.vector.tensor_copy(x_bf16[:, cb, :], x[:, cb, :])
-            nc.sync.dma_start(out_blocks[0, :, cb, :], x[:, cb, :])
+            if cb == BLOCKS - 2:
+                nc.sync.dma_start(out_blocks[0, :, 0 : BLOCKS - 1, :], x[:, 0 : BLOCKS - 1, :])
+            if cb == BLOCKS - 1:
+                nc.sync.dma_start(out_blocks[0, :, cb, :], x[:, cb, :])
             for g in (GROUP_Q, GROUP_K):
                 for fb in range(BLOCKS):
                     nc.tensor.matmul(
@@ -76,9 +81,12 @@ def tile_attentionbasedmodel_kernel(tc, emb, pe, qkv_w, qkv_b, offs, out):
                         start=(cb == 0),
                         stop=(cb == BLOCKS - 1),
                     )
-        for g in (GROUP_Q, GROUP_K):
-            for fb in range(BLOCKS):
-                add_bias_and_store(qk_acc[g][fb], g, fb)
+        for fb in range(BLOCKS):
+            add_bias(qk_acc[GROUP_Q][fb], GROUP_Q, fb)
+            store(GROUP_Q, fb, 1)
+        for fb in range(BLOCKS):
+            add_bias(qk_acc[GROUP_K][fb], GROUP_K, fb)
+        store(GROUP_K, 0, BLOCKS)
 
         for fb in range(BLOCKS):
             v_acc = banks.tile([P, N], F32, name=f"acc{GROUP_V}{fb}", tag="acc")
@@ -86,4 +94,5 @@ def tile_attentionbasedmodel_kernel(tc, emb, pe, qkv_w, qkv_b, offs, out):
                 nc.tensor.matmul(
                     v_acc[:], w_v_blocks[:, cb, fb, :], x_bf16[:, cb, :], start=(cb == 0), stop=(cb == BLOCKS - 1)
                 )
-            add_bias_and_store(v_acc, GROUP_V, fb)
+            add_bias(v_acc, GROUP_V, fb)
+            store(GROUP_V, fb, 1)

@@ -30,8 +30,8 @@ def tile_attentionbasedmodel_kernel(tc, emb, pe, qkv_w, qkv_b, offs, out):
         offsets = held.tile([P, N // OFFSETS_A_COLUMN], U16, name="offsets")
         nc.sync.dma_start(offsets[:], offs)
         table = [held.tile([P, V], F32, name=f"table{cb}") for cb in range(BLOCKS)]
-        pos = held.tile([P, BLOCKS, T], F32, name="pos")
-        nc.sync.dma_start(pos[:], pe_blocks[:, :, 0:T])
+        pos_once = held.tile([P, BLOCKS, T], F32, name="pos_once")
+        nc.sync.dma_start(pos_once[:], pe_blocks[:, :, 0:T])
         w_qk = [held.tile([P, 2 * D], BF16, name=f"w_qk{cb}") for cb in range(BLOCKS)]
         w_v = held.tile([P, BLOCKS, D], BF16, name="w_v")
         bias = held.tile([P, M // D, BLOCKS], F32, name="bias")
@@ -44,6 +44,7 @@ def tile_attentionbasedmodel_kernel(tc, emb, pe, qkv_w, qkv_b, offs, out):
         w_qk_blocks = [w_qk[cb][:].rearrange("p (g f i) -> p g i f", g=2, i=BLOCKS) for cb in range(BLOCKS)]
         w_v_blocks = w_v[:].rearrange("p c (f i) -> p c i f", i=BLOCKS)
 
+        pos = held.tile([P, BLOCKS, N], F32, name="pos")
         x = held.tile([P, BLOCKS, N], F32, name="x")
         x_bf16 = held.tile([P, BLOCKS, N], BF16, name="x_bf16")
         qkv = [held.tile([P, BLOCKS, N], F32, name=f"qkv{g}") for g in (GROUP_Q, GROUP_K, GROUP_V)]
@@ -62,11 +63,11 @@ def tile_attentionbasedmodel_kernel(tc, emb, pe, qkv_w, qkv_b, offs, out):
             for g in (GROUP_Q, GROUP_K)
         ]
         for cb in range(BLOCKS):
-            for s in range(N // T):
-                piece = offsets[:, s * (T // OFFSETS_A_COLUMN) : (s + 1) * (T // OFFSETS_A_COLUMN)]
-                nc.vector.tensor_tensor(
-                    x[:, cb, s * T : (s + 1) * T], table[cb][:].indirect(piece), pos[:, cb, :], ADD
-                )
+            nc.vector.tensor_copy(
+                pos[:, cb, :].rearrange("p (s t) -> p s t", t=T),
+                pos_once[:, cb, :].unsqueeze(1).to_broadcast([P, N // T, T]),
+            )
+            nc.vector.tensor_tensor(x[:, cb, :], table[cb][:].indirect(offsets[:]), pos[:, cb, :], ADD)
             nc.vector.tensor_copy(x_bf16[:, cb, :], x[:, cb, :])
             if cb == BLOCKS - 2:
                 nc.sync.dma_start(out_blocks[0, :, 0 : BLOCKS - 1, :], x[:, 0 : BLOCKS - 1, :])

@@ -31,7 +31,7 @@ def tile_attentionbasedmodel_kernel(tc, emb, pe, qkv_w, qkv_b, offs, out):
         nc.sync.dma_start(offsets[:], offs)
         table = [held.tile([P, V], F32, name=f"table{cb}") for cb in range(BLOCKS)]
         pos_once = held.tile([P, BLOCKS, T], F32, name="pos_once")
-        nc.sync.dma_start(pos_once[:], pe_blocks[:, :, 0:T])
+        nc.scalar.dma_start(pos_once[:], pe_blocks[:, :, 0:T])
         w_qk = [held.tile([P, 2 * D], BF16, name=f"w_qk{cb}") for cb in range(BLOCKS)]
         w_v = held.tile([P, BLOCKS, D], BF16, name="w_v")
         bias = held.tile([P, M // D, BLOCKS], F32, name="bias")

@@ -3,9 +3,13 @@ import concourse.mybir as mybir
 P = 128
 D, V, N, M = 512, 2048, 512, 1536
 T = 128
-BLOCKS = D // P
-GROUP_Q, GROUP_K, GROUP_V = 0, 1, 2
+CHANNEL_BLOCKS = D // P
+FEATURE_BLOCKS = M // P
+HALF = CHANNEL_BLOCKS // 2
 PSUM_BANKS = 8
+KEPT = range(0, 2 * PSUM_BANKS - FEATURE_BLOCKS)
+SET_ASIDE = range(2 * PSUM_BANKS - FEATURE_BLOCKS, PSUM_BANKS)
+LATE = range(PSUM_BANKS, FEATURE_BLOCKS)
 OFFSETS_A_COLUMN = 16
 F32, BF16, U16 = mybir.dt.float32, mybir.dt.bfloat16, mybir.dt.uint16
 ADD = mybir.AluOpType.add
@@ -17,11 +21,12 @@ BYTES = 4 * D * V + 4 * D * T + 2 * D * M + 4 * M + 2 * P * (N // OFFSETS_A_COLU
 
 def tile_attentionbasedmodel_kernel(tc, emb, pe, qkv_w, qkv_b, offs, out):
     nc = tc.nc
-    emb_blocks = emb.rearrange("(p i) v -> p i v", i=BLOCKS)
-    pe_blocks = pe.rearrange("(p i) j -> p i j", i=BLOCKS)
-    w_blocks = qkv_w.rearrange("(p i) m -> p i m", i=BLOCKS)
-    bias_blocks = qkv_b.rearrange("(g p i) o -> p g (i o)", p=P, i=BLOCKS)
-    out_blocks = out.rearrange("(g p i) j -> g p i j", p=P, i=BLOCKS)
+    emb_rows = emb.rearrange("(p c) v -> p c v", c=CHANNEL_BLOCKS)
+    pe_rows = pe.rearrange("(p c) j -> p c j", c=CHANNEL_BLOCKS)
+    w_rows = qkv_w.rearrange("(p c) m -> p c m", c=CHANNEL_BLOCKS)
+    bias_rows = qkv_b.rearrange("(p f) o -> p (f o)", f=FEATURE_BLOCKS)
+    x_rows = out[0:D, :].rearrange("(p c) j -> p c j", c=CHANNEL_BLOCKS)
+    qkv_rows = out[D : D + M, :].rearrange("(p f) j -> p f j", f=FEATURE_BLOCKS)
 
     with (
         tc.tile_pool(name="held", bufs=1) as held,
@@ -29,71 +34,77 @@ def tile_attentionbasedmodel_kernel(tc, emb, pe, qkv_w, qkv_b, offs, out):
     ):
         offsets = held.tile([P, N // OFFSETS_A_COLUMN], U16, name="offsets")
         nc.sync.dma_start(offsets[:], offs)
-        table = [held.tile([P, V], F32, name=f"table{cb}") for cb in range(BLOCKS)]
-        pos_once = held.tile([P, BLOCKS, T], F32, name="pos_once")
-        nc.scalar.dma_start(pos_once[:], pe_blocks[:, :, 0:T])
-        w_qk = [held.tile([P, 2 * D], BF16, name=f"w_qk{cb}") for cb in range(BLOCKS)]
-        w_v = held.tile([P, BLOCKS, D], BF16, name="w_v")
-        bias = held.tile([P, M // D, BLOCKS], F32, name="bias")
-        for cb in range(BLOCKS):
-            nc.sync.dma_start(table[cb][:], emb_blocks[:, cb, :])
-            nc.sync.dma_start(w_qk[cb][:], w_blocks[:, cb, 0 : 2 * D])
-        nc.sync.dma_start(bias[:], bias_blocks)
-        nc.sync.dma_start(w_v[:], w_blocks[:, :, 2 * D : M])
+        table = [held.tile([P, V], F32, name=f"table{cb}") for cb in range(CHANNEL_BLOCKS)]
+        pos_once = held.tile([P, CHANNEL_BLOCKS, T], F32, name="pos_once")
+        nc.scalar.dma_start(pos_once[:], pe_rows[:, :, 0:T])
+        weights = [held.tile([P, HALF, M], BF16, name=f"weights{h}") for h in range(2)]
+        bias = held.tile([P, FEATURE_BLOCKS], F32, name="bias")
+        nc.sync.dma_start(table[0][:], emb_rows[:, 0, :])
+        nc.sync.dma_start(weights[0][:], w_rows[:, 0:HALF, :])
+        nc.sync.dma_start(bias[:], bias_rows)
+        for cb in range(1, CHANNEL_BLOCKS):
+            nc.sync.dma_start(table[cb][:], emb_rows[:, cb, :])
+        nc.sync.dma_start(weights[1][:], w_rows[:, HALF:CHANNEL_BLOCKS, :])
 
-        w_qk_blocks = [w_qk[cb][:].rearrange("p (g f i) -> p g i f", g=2, i=BLOCKS) for cb in range(BLOCKS)]
-        w_v_blocks = w_v[:].rearrange("p c (f i) -> p c i f", i=BLOCKS)
+        w_blocks = [weights[h][:].rearrange("p c (m f) -> p c f m", f=FEATURE_BLOCKS) for h in range(2)]
 
-        pos = held.tile([P, BLOCKS, N], F32, name="pos")
-        x = held.tile([P, BLOCKS, N], F32, name="x")
-        x_bf16 = held.tile([P, BLOCKS, N], BF16, name="x_bf16")
-        qkv = [held.tile([P, BLOCKS, N], F32, name=f"qkv{g}") for g in (GROUP_Q, GROUP_K, GROUP_V)]
+        pos = held.tile([P, CHANNEL_BLOCKS, N], F32, name="pos")
+        x = held.tile([P, CHANNEL_BLOCKS, N], F32, name="x")
+        x_bf16 = held.tile([P, CHANNEL_BLOCKS, N], BF16, name="x_bf16")
+        half_sum = held.tile([P, len(SET_ASIDE), N], F32, name="half_sum")
+        qkv = held.tile([P, FEATURE_BLOCKS, N], F32, name="qkv")
+        acc = {}
 
-        def add_bias(acc, g, fb):
-            if fb % 2 == 0:
-                nc.scalar.activation(qkv[g][:, fb, :], acc[:], IDENTITY, bias=bias[:, g, fb : fb + 1])
-            else:
-                nc.vector.tensor_scalar_add(qkv[g][:, fb, :], acc[:], bias[:, g, fb : fb + 1])
-
-        def store(g, first, count):
-            nc.sync.dma_start(out_blocks[1 + g, :, first : first + count, :], qkv[g][:, first : first + count, :])
-
-        qk_acc = [
-            [banks.tile([P, N], F32, name=f"acc{g}{fb}", tag="acc") for fb in range(BLOCKS)]
-            for g in (GROUP_Q, GROUP_K)
-        ]
-        for cb in range(BLOCKS):
+        def look_up(cb):
             nc.vector.tensor_copy(
                 pos[:, cb, :].rearrange("p (s t) -> p s t", t=T),
                 pos_once[:, cb, :].unsqueeze(1).to_broadcast([P, N // T, T]),
             )
             nc.vector.tensor_tensor(x[:, cb, :], table[cb][:].indirect(offsets[:]), pos[:, cb, :], ADD)
             nc.vector.tensor_copy(x_bf16[:, cb, :], x[:, cb, :])
-            if cb == BLOCKS - 2:
-                nc.sync.dma_start(out_blocks[0, :, 0 : BLOCKS - 1, :], x[:, 0 : BLOCKS - 1, :])
-            if cb == BLOCKS - 1:
-                nc.sync.dma_start(out_blocks[0, :, cb, :], x[:, cb, :])
-            for g in (GROUP_Q, GROUP_K):
-                for fb in range(BLOCKS):
-                    nc.tensor.matmul(
-                        qk_acc[g][fb][:],
-                        w_qk_blocks[cb][:, g, fb, :],
-                        x_bf16[:, cb, :],
-                        start=(cb == 0),
-                        stop=(cb == BLOCKS - 1),
-                    )
-        for fb in range(BLOCKS):
-            add_bias(qk_acc[GROUP_Q][fb], GROUP_Q, fb)
-            store(GROUP_Q, fb, 1)
-        for fb in range(BLOCKS):
-            add_bias(qk_acc[GROUP_K][fb], GROUP_K, fb)
-        store(GROUP_K, 0, BLOCKS)
+            if cb == CHANNEL_BLOCKS - 2:
+                nc.sync.dma_start(x_rows[:, 0 : CHANNEL_BLOCKS - 1, :], x[:, 0 : CHANNEL_BLOCKS - 1, :])
+            if cb == CHANNEL_BLOCKS - 1:
+                nc.sync.dma_start(x_rows[:, cb, :], x[:, cb, :])
 
-        for fb in range(BLOCKS):
-            v_acc = banks.tile([P, N], F32, name=f"acc{GROUP_V}{fb}", tag="acc")
-            for cb in range(BLOCKS):
-                nc.tensor.matmul(
-                    v_acc[:], w_v_blocks[:, cb, fb, :], x_bf16[:, cb, :], start=(cb == 0), stop=(cb == BLOCKS - 1)
-                )
-            add_bias(v_acc, GROUP_V, fb)
-            store(GROUP_V, fb, 1)
+        def new_bank(fb):
+            acc[fb] = banks.tile([P, N], F32, name=f"acc{fb}_{len(acc)}", tag="acc")
+
+        def multiply(fb, cb, first, last):
+            nc.tensor.matmul(
+                acc[fb][:], w_blocks[cb // HALF][:, cb % HALF, fb, :], x_bf16[:, cb, :], start=first, stop=last
+            )
+
+        for fb in list(SET_ASIDE) + list(KEPT):
+            new_bank(fb)
+        look_up(0)
+        for fb in list(SET_ASIDE) + list(KEPT):
+            multiply(fb, 0, first=True, last=False)
+        look_up(1)
+        for fb in SET_ASIDE:
+            multiply(fb, 1, first=False, last=True)
+        for fb in KEPT:
+            multiply(fb, 1, first=False, last=False)
+        for fb in SET_ASIDE:
+            nc.scalar.activation(
+                half_sum[:, fb - SET_ASIDE.start, :], acc[fb][:], IDENTITY, bias=bias[:, fb : fb + 1]
+            )
+        for fb in LATE:
+            new_bank(fb)
+            multiply(fb, 0, first=True, last=False)
+            multiply(fb, 1, first=False, last=False)
+        look_up(2)
+        look_up(3)
+
+        for fb in range(FEATURE_BLOCKS):
+            if fb in SET_ASIDE:
+                new_bank(fb)
+            multiply(fb, 2, first=(fb in SET_ASIDE), last=False)
+            multiply(fb, 3, first=False, last=True)
+            if fb in SET_ASIDE:
+                nc.vector.tensor_tensor(qkv[:, fb, :], acc[fb][:], half_sum[:, fb - SET_ASIDE.start, :], ADD)
+            elif fb % 2 == 0:
+                nc.scalar.activation(qkv[:, fb, :], acc[fb][:], IDENTITY, bias=bias[:, fb : fb + 1])
+            else:
+                nc.vector.tensor_scalar_add(qkv[:, fb, :], acc[fb][:], bias[:, fb : fb + 1])
+            nc.sync.dma_start(qkv_rows[:, fb, :], qkv[:, fb, :])

import concourse.mybir as mybir

P = 128
D, V, N, M = 512, 2048, 512, 1536
T = 128
CHANNEL_BLOCKS = D // P
FEATURE_BLOCKS = M // P
HALF = CHANNEL_BLOCKS // 2
PSUM_BANKS = 8
KEPT = range(0, 2 * PSUM_BANKS - FEATURE_BLOCKS)
SET_ASIDE = range(2 * PSUM_BANKS - FEATURE_BLOCKS, PSUM_BANKS)
LATE = range(PSUM_BANKS, FEATURE_BLOCKS)
OFFSETS_A_COLUMN = 16
F32, BF16, U16 = mybir.dt.float32, mybir.dt.bfloat16, mybir.dt.uint16
ADD = mybir.AluOpType.add
IDENTITY = mybir.ActivationFunctionType.Identity

FLOPS = 2 * D * M * N
BYTES = 4 * D * V + 4 * D * T + 2 * D * M + 4 * M + 2 * P * (N // OFFSETS_A_COLUMN) + 4 * (D + M) * N


def tile_attentionbasedmodel_kernel(tc, emb, pe, qkv_w, qkv_b, offs, out):
    nc = tc.nc
    emb_rows = emb.rearrange("(p c) v -> p c v", c=CHANNEL_BLOCKS)
    pe_rows = pe.rearrange("(p c) j -> p c j", c=CHANNEL_BLOCKS)
    w_rows = qkv_w.rearrange("(p c) m -> p c m", c=CHANNEL_BLOCKS)
    bias_rows = qkv_b.rearrange("(p f) o -> p (f o)", f=FEATURE_BLOCKS)
    x_rows = out[0:D, :].rearrange("(p c) j -> p c j", c=CHANNEL_BLOCKS)
    qkv_rows = out[D : D + M, :].rearrange("(p f) j -> p f j", f=FEATURE_BLOCKS)

    with (
        tc.tile_pool(name="held", bufs=1) as held,
        tc.psum_pool(name="banks", bufs=PSUM_BANKS) as banks,
    ):
        offsets = held.tile([P, N // OFFSETS_A_COLUMN], U16, name="offsets")
        nc.sync.dma_start(offsets[:], offs)
        table = [held.tile([P, V], F32, name=f"table{cb}") for cb in range(CHANNEL_BLOCKS)]
        pos_once = held.tile([P, CHANNEL_BLOCKS, T], F32, name="pos_once")
        nc.scalar.dma_start(pos_once[:], pe_rows[:, :, 0:T])
        weights = [held.tile([P, HALF, M], BF16, name=f"weights{h}") for h in range(2)]
        bias = held.tile([P, FEATURE_BLOCKS], F32, name="bias")
        nc.sync.dma_start(table[0][:], emb_rows[:, 0, :])
        nc.sync.dma_start(weights[0][:], w_rows[:, 0:HALF, :])
        nc.sync.dma_start(bias[:], bias_rows)
        for cb in range(1, CHANNEL_BLOCKS):
            nc.sync.dma_start(table[cb][:], emb_rows[:, cb, :])
        nc.sync.dma_start(weights[1][:], w_rows[:, HALF:CHANNEL_BLOCKS, :])

        w_blocks = [weights[h][:].rearrange("p c (m f) -> p c f m", f=FEATURE_BLOCKS) for h in range(2)]

        pos = held.tile([P, CHANNEL_BLOCKS, N], F32, name="pos")
        x = held.tile([P, CHANNEL_BLOCKS, N], F32, name="x")
        x_bf16 = held.tile([P, CHANNEL_BLOCKS, N], BF16, name="x_bf16")
        half_sum = held.tile([P, len(SET_ASIDE), N], F32, name="half_sum")
        qkv = held.tile([P, FEATURE_BLOCKS, N], F32, name="qkv")
        acc = {}

        def look_up(cb):
            nc.vector.tensor_copy(
                pos[:, cb, :].rearrange("p (s t) -> p s t", t=T),
                pos_once[:, cb, :].unsqueeze(1).to_broadcast([P, N // T, T]),
            )
            nc.vector.tensor_tensor(x[:, cb, :], table[cb][:].indirect(offsets[:]), pos[:, cb, :], ADD)
            nc.vector.tensor_copy(x_bf16[:, cb, :], x[:, cb, :])
            if cb == CHANNEL_BLOCKS - 2:
                nc.sync.dma_start(x_rows[:, 0 : CHANNEL_BLOCKS - 1, :], x[:, 0 : CHANNEL_BLOCKS - 1, :])
            if cb == CHANNEL_BLOCKS - 1:
                nc.sync.dma_start(x_rows[:, cb, :], x[:, cb, :])

        def new_bank(fb):
            acc[fb] = banks.tile([P, N], F32, name=f"acc{fb}_{len(acc)}", tag="acc")

        def multiply(fb, cb, first, last):
            nc.tensor.matmul(
                acc[fb][:], w_blocks[cb // HALF][:, cb % HALF, fb, :], x_bf16[:, cb, :], start=first, stop=last
            )

        for fb in list(SET_ASIDE) + list(KEPT):
            new_bank(fb)
        look_up(0)
        for fb in list(SET_ASIDE) + list(KEPT):
            multiply(fb, 0, first=True, last=False)
        look_up(1)
        for fb in SET_ASIDE:
            multiply(fb, 1, first=False, last=True)
        for fb in KEPT:
            multiply(fb, 1, first=False, last=False)
        for fb in SET_ASIDE:
            nc.scalar.activation(
                half_sum[:, fb - SET_ASIDE.start, :], acc[fb][:], IDENTITY, bias=bias[:, fb : fb + 1]
            )
        for fb in LATE:
            new_bank(fb)
            multiply(fb, 0, first=True, last=False)
            multiply(fb, 1, first=False, last=False)
        look_up(2)
        look_up(3)

        for fb in range(FEATURE_BLOCKS):
            if fb in SET_ASIDE:
                new_bank(fb)
            multiply(fb, 2, first=(fb in SET_ASIDE), last=False)
            multiply(fb, 3, first=False, last=True)
            if fb in SET_ASIDE:
                nc.vector.tensor_tensor(qkv[:, fb, :], acc[fb][:], half_sum[:, fb - SET_ASIDE.start, :], ADD)
            elif fb % 2 == 0:
                nc.scalar.activation(qkv[:, fb, :], acc[fb][:], IDENTITY, bias=bias[:, fb : fb + 1])
            else:
                nc.vector.tensor_scalar_add(qkv[:, fb, :], acc[fb][:], bias[:, fb : fb + 1])
            nc.sync.dma_start(qkv_rows[:, fb, :], qkv[:, fb, :])
